import numpy as np
import ml_dtypes


def mxq(x, axis, fmt="e4m3"):
    dtype, down = {"e4m3": (ml_dtypes.float8_e4m3fn, 7), "e5m2": (ml_dtypes.float8_e5m2, 14)}[fmt]
    v = np.moveaxis(np.asarray(x, np.float32).astype(ml_dtypes.bfloat16).astype(np.float64), axis, -1)
    blocks = v.reshape(v.shape[:-1] + (-1, 32))
    amax = np.abs(blocks).max(-1, keepdims=True)
    byte = np.maximum(np.where(amax > 0, np.frexp(amax)[1] - 1 + 127, 0) - down, 1)
    scale = np.exp2(byte - 127.0)
    codes = (blocks / scale).astype(np.float32).astype(dtype).astype(np.float64)
    return np.moveaxis((codes * scale).reshape(v.shape), -1, axis)


WIDE = False


def mx_kscale(k):
    if not WIDE:
        return np.ones(k)
    levels = np.array([10, -10, 5, -5, 0])
    a = np.random.permutation(np.resize(levels, k // 512 * 4)).reshape(k // 512, 4)
    idx = np.arange(k)
    return np.exp2(a[idx // 512, idx % 128 // 32])


BF16 = ml_dtypes.bfloat16


def bf(x):
    return np.asarray(x, np.float32).astype(BF16)


def f64(x):
    return np.asarray(x).astype(np.float64)


E2M1 = np.array([0.0, 0.5, 1.0, 1.5, 2.0, 3.0, 4.0, 6.0, -0.0, -0.5, -1.0, -1.5, -2.0, -3.0, -4.0, -6.0])


def pack_weight(w, fmt):
    k, n = w.shape
    w = f64(bf(w)).reshape(k // 32, 32, n)
    amax = np.abs(w).max(1)
    if fmt == "e4m3":
        byte = np.frexp(amax)[1] - 1 + 127 - 7
    else:
        mant, ex = np.frexp(amax / 6.0)
        byte = np.where(mant > 0.5, ex, ex - 1) + 127
    byte = np.clip(np.where(amax > 0, byte, 1), 1, 254)
    scaled = (w * np.exp2(127.0 - byte)[:, None, :]).reshape(k, n).astype(np.float32)
    by_word = np.ascontiguousarray(scaled.reshape(k // 512, 128, 4, n).transpose(0, 1, 3, 2))
    if fmt == "e4m3":
        words = by_word.astype(ml_dtypes.float8_e4m3fn).view(np.uint8)
    else:
        c = by_word.astype(ml_dtypes.float4_e2m1fn).view(np.uint8) & 0xF
        words = c[..., 0::2] | (c[..., 1::2] << 4)
    return np.ascontiguousarray(words), np.ascontiguousarray(byte.astype(np.uint8).reshape(k // 512, 16, n))


def unpack_weight(words, scales, fmt):
    g, p, n, _ = words.shape
    if fmt == "e4m3":
        vals = np.ascontiguousarray(words).view(ml_dtypes.float8_e4m3fn).astype(np.float64)
    else:
        nib = np.empty((g, p, n, 4), np.uint8)
        nib[..., 0::2] = words & 0xF
        nib[..., 1::2] = words >> 4
        vals = E2M1[nib]
    vals = vals * np.repeat(np.exp2(scales.astype(np.float64) - 127.0), 8, axis=1)[..., None]
    return vals.transpose(0, 1, 3, 2).reshape(g * 512, n)


T, BLK, B, NH, NW, C, K = 16, 4, 4, 8, 8, 512, 1024
R = B * NH * NW
HAD = np.array([[1.0, 1.0, 1.0, 1.0],
                [1.0, -1.0, 1.0, -1.0],
                [1.0, 1.0, -1.0, -1.0],
                [1.0, -1.0, -1.0, 1.0]])


def setup_inputs():
    s = mx_kscale(C)
    trans = bf(np.random.standard_normal((T, B, NH, NW, C)) * s)
    stack = np.random.standard_normal((T, C, K)) * 2.0 / np.sqrt(C) / s[None, :, None]
    words, scales = pack_weight(stack.reshape(-1, K), "e4m3")
    bias = bf(np.random.standard_normal((1, 1, 1, K)) * 0.2)
    return {"trans": trans,
            "weight_words": words,
            "weight_scales": scales,
            "bias": bias}


def reference(trans, weight_words, weight_scales, bias):
    mixed = mxq(f64(trans).reshape(T, R, C), 2, "e4m3") @ unpack_weight(weight_words, weight_scales, "e4m3").reshape(T, C, K)
    mixed = mixed.reshape(BLK, BLK, B, NH, NW, K)
    out = np.zeros((B, NH, BLK, NW, BLK, K))
    for i in range(BLK):
        for j in range(BLK):
            acc = np.zeros((B, NH, NW, K))
            for u in range(BLK):
                for v in range(BLK):
                    acc = acc + HAD[i, u] * HAD[j, v] * mixed[u, v]
            out[:, :, i, :, j, :] = acc
    out = out * (1.0 / T)
    return out.reshape(B, NH * BLK, NW * BLK, K) + f64(bias)

@@ -1,0 +1,165 @@
+from contextlib import ExitStack
+
+import concourse.mybir as mybir
+from concourse.masks import make_identity
+
+F32 = mybir.dt.float32
+BF16 = mybir.dt.bfloat16
+I32 = mybir.dt.int32
+U32 = mybir.dt.uint32
+U8 = mybir.dt.uint8
+FP8X4 = mybir.dt.float8_e4m3fn_x4
+ADD = mybir.AluOpType.add
+SUBTRACT = mybir.AluOpType.subtract
+MULT = mybir.AluOpType.mult
+
+P = 128
+PACK = 4
+BLK = 4
+COEFFS = BLK * BLK
+ROWS = 256
+ROW_TILES = ROWS // P
+BLOCK_COLS = 8
+CHANNELS = 512
+OUT_CHANNELS = 1024
+N_TILE = 512
+COL_TILES = OUT_CHANNELS // N_TILE
+QUADRANT = 32
+HADAMARD = ((1, 1, 1, 1), (1, -1, 1, -1), (1, 1, -1, -1), (1, -1, -1, 1))
+PLUS = 0
+MINUS = 1
+J_GROUP = 2
+
+FLOPS = 2 * COEFFS * ROWS * CHANNELS * OUT_CHANNELS
+
+
+def tile_iwht2layer_pa_t_e_kernel(tc, trans, weight_words, weight_scales, bias, out):
+    nc = tc.nc
+
+    x_dram = trans.rearrange("t b h w c -> (b h w) t c")
+    w_dram = weight_words.rearrange("g p n t -> p g (n t)")
+    out_dram = out.rearrange("b (h i) (w j) n -> i j (b h) w n", i=BLK, j=BLK)
+
+    with ExitStack() as stack:
+        keep = stack.enter_context(tc.tile_pool(name="keep", bufs=1))
+        prep = stack.enter_context(tc.tile_pool(name="prep", bufs=2))
+        evens = stack.enter_context(tc.tile_pool(name="evens", bufs=6))
+        sums = stack.enter_context(tc.tile_pool(name="sums", bufs=3))
+        outs = stack.enter_context(tc.tile_pool(name="outs", bufs=4))
+        psum = stack.enter_context(tc.psum_pool(name="psum", bufs=8))
+        stack.enter_context(tc.manual_schedule())
+
+        x_raw = keep.tile([P, ROW_TILES, COEFFS, CHANNELS], BF16)
+        x_codes = keep.tile([P, ROW_TILES, BLK, 2, BLK, P], U32, align_bytes=64)
+        x_scales = keep.tile([P, ROW_TILES, BLK, 2, BLK, P], U8, align_bytes=64)
+        w_codes = keep.tile([P, COEFFS, OUT_CHANNELS], U32, align_bytes=64)
+        w_scales = keep.tile([P, BLK, OUT_CHANNELS], U8, align_bytes=64)
+        nc.vector.memset(w_scales[:].bitcast(I32), 0)
+        identity = keep.tile([P, P], F32)
+        make_identity(nc, identity[:])
+        bias_rows = keep.tile([P, OUT_CHANNELS], BF16)
+        nc.scalar.dma_start(
+            out=bias_rows[:], in_=bias.rearrange("a b c n -> (a b c n)").partition_broadcast(P)
+        )
+
+        for m in range(ROW_TILES):
+            for u in range(BLK):
+                coeffs = slice(BLK * u, BLK * (u + 1))
+                nc.sync.dma_start(out=x_raw[:, m, coeffs, :], in_=x_dram[m * P : (m + 1) * P, coeffs, :])
+        for u in range(BLK):
+            for quadrant in range(P // QUADRANT):
+                nc.sync.dma_start(
+                    out=w_scales[QUADRANT * quadrant : QUADRANT * quadrant + BLK * PACK, u, :].bitcast(I32),
+                    in_=weight_scales[
+                        BLK * u : BLK * (u + 1), PACK * quadrant : PACK * (quadrant + 1), :
+                    ].bitcast(I32),
+                )
+        for n in range(COL_TILES):
+            for u in range(BLK):
+                coeffs = slice(BLK * u, BLK * (u + 1))
+                nc.sync.dma_start(
+                    out=w_codes[:, coeffs, n * N_TILE : (n + 1) * N_TILE].bitcast(I32),
+                    in_=w_dram[:, coeffs, n * N_TILE * PACK : (n + 1) * N_TILE * PACK].bitcast(I32),
+                )
+
+        for m in range(ROW_TILES):
+            for u in range(BLK):
+                grouped = prep.tile([P, 2, BLK, P, PACK], BF16, align_bytes=64)
+                for first_v in range(0, BLK, 2):
+                    flipped = psum.tile([P, 2, 2, P], F32, tag="bank")
+                    for c in range(2):
+                        words = x_raw[:, m, BLK * u + first_v + c, :].bitcast(F32)
+                        for e in range(2):
+                            nc.tensor.transpose(
+                                flipped[:, c, e, :], words[:, e : CHANNELS // 2 : 2], identity[:]
+                            )
+                    nc.scalar.copy(
+                        out=grouped[:, PLUS, first_v : first_v + 2].bitcast(F32),
+                        in_=flipped[:].rearrange("p c e r -> p c r e"),
+                    )
+                nc.vector.tensor_scalar_mul(
+                    out=grouped[:, MINUS].rearrange("p v r t -> p (v r t)"),
+                    in0=grouped[:, PLUS].rearrange("p v r t -> p (v r t)"),
+                    scalar1=-1.0,
+                )
+                nc.vector.quantize_mx(
+                    out=x_codes[:, m, u].rearrange("p s v r -> p (s v r)").bitcast(FP8X4),
+                    scales=x_scales[:, m, u].rearrange("p s v r -> p (s v r)"),
+                    in_=grouped[:].rearrange("p s v r t -> p (s v r t)"),
+                )
+
+        for n in range(COL_TILES):
+            cols = slice(n * N_TILE, (n + 1) * N_TILE)
+            for m in range(ROW_TILES):
+                block_rows = slice(m * P // BLOCK_COLS, (m + 1) * P // BLOCK_COLS)
+                for first_j in range(0, BLK, J_GROUP):
+                    even = {}
+                    stage_a = {}
+                    for u in range(BLK):
+                        for j in range(first_j, first_j + J_GROUP):
+                            part = psum.tile([P, N_TILE], F32, tag="bank")
+                            for v in range(BLK):
+                                sign = PLUS if HADAMARD[j][v] > 0 else MINUS
+                                nc.tensor.matmul_mx(
+                                    out=part[:],
+                                    lhsT=x_codes[:, m, u, sign, v, :].bitcast(FP8X4),
+                                    lhsT_scale=x_scales[:, m, u, sign, v, :],
+                                    rhs=w_codes[:, BLK * u + v, cols].bitcast(FP8X4),
+                                    rhs_scale=w_scales[PACK * v : P, u, cols],
+                                    start=(v == 0),
+                                    stop=(v == BLK - 1),
+                                )
+                            if u % 2 == 0:
+                                scaled = evens.tile([P, N_TILE], F32)
+                                nc.scalar.mul(out=scaled[:], in_=part[:], mul=1.0 / COEFFS)
+                                if u == 0:
+                                    nc.gpsimd.tensor_tensor(
+                                        out=scaled[:], in0=scaled[:], in1=bias_rows[:, cols], op=ADD
+                                    )
+                                even[j] = scaled
+                            else:
+                                both = sums.tile([P, 2, N_TILE], F32, tag="stage_a%d" % (u // 2))
+                                nc.vector.scalar_tensor_tensor(
+                                    out=both[:, 0, :], in0=part[:], scalar=1.0 / COEFFS,
+                                    in1=even[j][:], op0=MULT, op1=ADD,
+                                )
+                                nc.vector.scalar_tensor_tensor(
+                                    out=both[:, 1, :], in0=part[:], scalar=-1.0 / COEFFS,
+                                    in1=even[j][:], op0=MULT, op1=ADD,
+                                )
+                                stage_a[(j, u // 2)] = both
+                            if u == BLK - 1:
+                                upper = outs.tile([P, 2, N_TILE], F32)
+                                lower = outs.tile([P, 2, N_TILE], F32)
+                                nc.vector.tensor_tensor(
+                                    out=upper[:], in0=stage_a[(j, 0)][:], in1=stage_a[(j, 1)][:], op=ADD
+                                )
+                                helper = nc.gpsimd if j % 2 == 1 else nc.vector
+                                helper.tensor_tensor(
+                                    out=lower[:], in0=stage_a[(j, 0)][:], in1=stage_a[(j, 1)][:], op=SUBTRACT
+                                )
+                                for i in range(BLK):
+                                    pixels = (upper, lower)[i // 2]
+                                    nc.sync.dma_start(
+                                        out=out_dram[i, j, block_rows, :, cols], in_=pixels[:, i % 2, :]
+                                    )

@@ -131,11 +131,13 @@ def tile_iwht2layer_pa_t_e_kernel(tc, trans, weight_words, weight_scales, bias, 
                                 )
                             if u % 2 == 0:
                                 scaled = evens.tile([P, N_TILE], F32)
-                                nc.scalar.mul(out=scaled[:], in_=part[:], mul=1.0 / COEFFS)
                                 if u == 0:
-                                    nc.gpsimd.tensor_tensor(
-                                        out=scaled[:], in0=scaled[:], in1=bias_rows[:, cols], op=ADD
+                                    nc.vector.scalar_tensor_tensor(
+                                        out=scaled[:], in0=part[:], scalar=1.0 / COEFFS,
+                                        in1=bias_rows[:, cols], op0=MULT, op1=ADD,
                                     )
+                                else:
+                                    nc.scalar.mul(out=scaled[:], in_=part[:], mul=1.0 / COEFFS)
                                 even[j] = scaled
                             else:
                                 both = sums.tile([P, 2, N_TILE], F32, tag="stage_a%d" % (u // 2))
@@ -154,8 +156,7 @@ def tile_iwht2layer_pa_t_e_kernel(tc, trans, weight_words, weight_scales, bias, 
                                 nc.vector.tensor_tensor(
                                     out=upper[:], in0=stage_a[(j, 0)][:], in1=stage_a[(j, 1)][:], op=ADD
                                 )
-                                helper = nc.gpsimd if j % 2 == 1 else nc.vector
-                                helper.tensor_tensor(
+                                nc.gpsimd.tensor_tensor(
                                     out=lower[:], in0=stage_a[(j, 0)][:], in1=stage_a[(j, 1)][:], op=SUBTRACT
                                 )
                                 for i in range(BLK):

@@ -153,10 +153,11 @@ def tile_iwht2layer_pa_t_e_kernel(tc, trans, weight_words, weight_scales, bias, 
                             if u == BLK - 1:
                                 upper = outs.tile([P, 2, N_TILE], F32)
                                 lower = outs.tile([P, 2, N_TILE], F32)
-                                nc.vector.tensor_tensor(
+                                adder = nc.vector if j % 2 == 0 else nc.gpsimd
+                                adder.tensor_tensor(
                                     out=upper[:], in0=stage_a[(j, 0)][:], in1=stage_a[(j, 1)][:], op=ADD
                                 )
-                                nc.gpsimd.tensor_tensor(
+                                adder.tensor_tensor(
                                     out=lower[:], in0=stage_a[(j, 0)][:], in1=stage_a[(j, 1)][:], op=SUBTRACT
                                 )
                                 for i in range(BLK):

@@ -19,7 +19,6 @@ BLK = 4
 COEFFS = BLK * BLK
 ROWS = 256
 ROW_TILES = ROWS // P
-BLOCK_COLS = 8
 CHANNELS = 512
 OUT_CHANNELS = 1024
 N_TILE = 512
@@ -36,9 +35,9 @@ FLOPS = 2 * COEFFS * ROWS * CHANNELS * OUT_CHANNELS
 def tile_iwht2layer_pa_t_e_kernel(tc, trans, weight_words, weight_scales, bias, out):
     nc = tc.nc
 
-    x_dram = trans.rearrange("t b h w c -> (b h w) t c")
+    x_dram = trans.rearrange("t b h (w m) c -> (b h w) t (m c)", m=ROW_TILES)
     w_dram = weight_words.rearrange("g p n t -> p g (n t)")
-    out_dram = out.rearrange("b (h i) (w j) n -> i j (b h) w n", i=BLK, j=BLK)
+    out_dram = out.rearrange("b (h i) (w m j) n -> i j m (b h) w n", i=BLK, m=ROW_TILES, j=BLK)
 
     with ExitStack() as stack:
         keep = stack.enter_context(tc.tile_pool(name="keep", bufs=1))
@@ -49,7 +48,7 @@ def tile_iwht2layer_pa_t_e_kernel(tc, trans, weight_words, weight_scales, bias, 
         psum = stack.enter_context(tc.psum_pool(name="psum", bufs=8))
         stack.enter_context(tc.manual_schedule())
 
-        x_raw = keep.tile([P, ROW_TILES, COEFFS, CHANNELS], BF16)
+        x_raw = keep.tile([P, COEFFS, ROW_TILES, CHANNELS], BF16)
         x_codes = keep.tile([P, ROW_TILES, BLK, 2, BLK, P], U32, align_bytes=64)
         x_scales = keep.tile([P, ROW_TILES, BLK, 2, BLK, P], U8, align_bytes=64)
         w_codes = keep.tile([P, COEFFS, OUT_CHANNELS], U32, align_bytes=64)
@@ -57,15 +56,18 @@ def tile_iwht2layer_pa_t_e_kernel(tc, trans, weight_words, weight_scales, bias, 
         nc.vector.memset(w_scales[:].bitcast(I32), 0)
         identity = keep.tile([P, P], F32)
         make_identity(nc, identity[:])
-        bias_rows = keep.tile([P, OUT_CHANNELS], BF16)
-        nc.scalar.dma_start(
-            out=bias_rows[:], in_=bias.rearrange("a b c n -> (a b c n)").partition_broadcast(P)
-        )
+        bias_row0 = keep.tile([P, OUT_CHANNELS], BF16)
+        nc.gpsimd.memset(bias_row0[:], 0.0)
+        ones = keep.tile([P, P], BF16)
+        nc.gpsimd.memset(ones[:], 1.0)
 
-        for m in range(ROW_TILES):
-            for u in range(BLK):
-                coeffs = slice(BLK * u, BLK * (u + 1))
-                nc.sync.dma_start(out=x_raw[:, m, coeffs, :], in_=x_dram[m * P : (m + 1) * P, coeffs, :])
+        nc.scalar.dma_start(out=bias_row0[0:1, :], in_=bias.rearrange("a b c n -> (a b c) n"))
+
+        for u in range(BLK):
+            coeffs = slice(BLK * u, BLK * (u + 1))
+            nc.sync.dma_start(
+                out=x_raw[:, coeffs].rearrange("p t m c -> p t (m c)"), in_=x_dram[:, coeffs, :]
+            )
         for u in range(BLK):
             for quadrant in range(P // QUADRANT):
                 nc.sync.dma_start(
@@ -82,13 +84,13 @@ def tile_iwht2layer_pa_t_e_kernel(tc, trans, weight_words, weight_scales, bias, 
                     in_=w_dram[:, coeffs, n * N_TILE * PACK : (n + 1) * N_TILE * PACK].bitcast(I32),
                 )
 
-        for m in range(ROW_TILES):
-            for u in range(BLK):
+        for u in range(BLK):
+            for m in range(ROW_TILES):
                 grouped = prep.tile([P, 2, BLK, P, PACK], BF16, align_bytes=64)
                 for first_v in range(0, BLK, 2):
                     flipped = psum.tile([P, 2, 2, P], F32, tag="bank")
                     for c in range(2):
-                        words = x_raw[:, m, BLK * u + first_v + c, :].bitcast(F32)
+                        words = x_raw[:, BLK * u + first_v + c, m, :].bitcast(F32)
                         for e in range(2):
                             nc.tensor.transpose(
                                 flipped[:, c, e, :], words[:, e : CHANNELS // 2 : 2], identity[:]
@@ -108,10 +110,16 @@ def tile_iwht2layer_pa_t_e_kernel(tc, trans, weight_words, weight_scales, bias, 
                     in_=grouped[:].rearrange("p s v r t -> p (s v r t)"),
                 )
 
+        bias_rows = keep.tile([P, OUT_CHANNELS], F32)
+        for n in range(COL_TILES):
+            cols = slice(n * N_TILE, (n + 1) * N_TILE)
+            spread = psum.tile([P, N_TILE], F32, tag="bank")
+            nc.tensor.matmul(out=spread[:], lhsT=ones[:], rhs=bias_row0[:, cols], start=True, stop=True)
+            nc.scalar.copy(out=bias_rows[:, cols], in_=spread[:])
+
         for n in range(COL_TILES):
             cols = slice(n * N_TILE, (n + 1) * N_TILE)
             for m in range(ROW_TILES):
-                block_rows = slice(m * P // BLOCK_COLS, (m + 1) * P // BLOCK_COLS)
                 for first_j in range(0, BLK, J_GROUP):
                     even = {}
                     stage_a = {}
@@ -153,15 +161,14 @@ def tile_iwht2layer_pa_t_e_kernel(tc, trans, weight_words, weight_scales, bias, 
                             if u == BLK - 1:
                                 upper = outs.tile([P, 2, N_TILE], F32)
                                 lower = outs.tile([P, 2, N_TILE], F32)
-                                adder = nc.vector if j % 2 == 0 else nc.gpsimd
-                                adder.tensor_tensor(
+                                nc.vector.tensor_tensor(
                                     out=upper[:], in0=stage_a[(j, 0)][:], in1=stage_a[(j, 1)][:], op=ADD
                                 )
-                                adder.tensor_tensor(
+                                nc.gpsimd.tensor_tensor(
                                     out=lower[:], in0=stage_a[(j, 0)][:], in1=stage_a[(j, 1)][:], op=SUBTRACT
                                 )
                                 for i in range(BLK):
                                     pixels = (upper, lower)[i // 2]
                                     nc.sync.dma_start(
-                                        out=out_dram[i, j, block_rows, :, cols], in_=pixels[:, i % 2, :]
+                                        out=out_dram[i, j, m, :, :, cols], in_=pixels[:, i % 2, :]
                                     )

@@ -68,7 +68,6 @@ def tile_iwht2layer_pa_t_e_kernel(tc, trans, weight_words, weight_scales, bias, 
             nc.sync.dma_start(
                 out=x_raw[:, coeffs].rearrange("p t m c -> p t (m c)"), in_=x_dram[:, coeffs, :]
             )
-        for u in range(BLK):
             for quadrant in range(P // QUADRANT):
                 nc.sync.dma_start(
                     out=w_scales[QUADRANT * quadrant : QUADRANT * quadrant + BLK * PACK, u, :].bitcast(I32),
@@ -104,11 +103,12 @@ def tile_iwht2layer_pa_t_e_kernel(tc, trans, weight_words, weight_scales, bias, 
                     in0=grouped[:, PLUS].rearrange("p v r t -> p (v r t)"),
                     scalar1=-1.0,
                 )
-                nc.vector.quantize_mx(
-                    out=x_codes[:, m, u].rearrange("p s v r -> p (s v r)").bitcast(FP8X4),
-                    scales=x_scales[:, m, u].rearrange("p s v r -> p (s v r)"),
-                    in_=grouped[:].rearrange("p s v r t -> p (s v r t)"),
-                )
+                for sign in (PLUS, MINUS):
+                    nc.vector.quantize_mx(
+                        out=x_codes[:, m, u, sign].rearrange("p v r -> p (v r)").bitcast(FP8X4),
+                        scales=x_scales[:, m, u, sign].rearrange("p v r -> p (v r)"),
+                        in_=grouped[:, sign].rearrange("p v r t -> p (v r t)"),
+                    )
 
         bias_rows = keep.tile([P, OUT_CHANNELS], F32)
         for n in range(COL_TILES):
@@ -158,17 +158,15 @@ def tile_iwht2layer_pa_t_e_kernel(tc, trans, weight_words, weight_scales, bias, 
                                     in1=even[j][:], op0=MULT, op1=ADD,
                                 )
                                 stage_a[(j, u // 2)] = both
-                            if u == BLK - 1:
-                                upper = outs.tile([P, 2, N_TILE], F32)
-                                lower = outs.tile([P, 2, N_TILE], F32)
-                                nc.vector.tensor_tensor(
-                                    out=upper[:], in0=stage_a[(j, 0)][:], in1=stage_a[(j, 1)][:], op=ADD
-                                )
-                                nc.gpsimd.tensor_tensor(
-                                    out=lower[:], in0=stage_a[(j, 0)][:], in1=stage_a[(j, 1)][:], op=SUBTRACT
-                                )
-                                for i in range(BLK):
-                                    pixels = (upper, lower)[i // 2]
-                                    nc.sync.dma_start(
-                                        out=out_dram[i, j, m, :, :, cols], in_=pixels[:, i % 2, :]
-                                    )
+                    for j in range(first_j, first_j + J_GROUP):
+                        upper = outs.tile([P, 2, N_TILE], F32)
+                        lower = outs.tile([P, 2, N_TILE], F32)
+                        nc.vector.tensor_tensor(
+                            out=upper[:], in0=stage_a[(j, 0)][:], in1=stage_a[(j, 1)][:], op=ADD
+                        )
+                        nc.gpsimd.tensor_tensor(
+                            out=lower[:], in0=stage_a[(j, 0)][:], in1=stage_a[(j, 1)][:], op=SUBTRACT
+                        )
+                        for i in range(BLK):
+                            pixels = (upper, lower)[i // 2]
+                            nc.sync.dma_start(out=out_dram[i, j, m, :, :, cols], in_=pixels[:, i % 2, :])

@@ -42,9 +42,9 @@ def tile_iwht2layer_pa_t_e_kernel(tc, trans, weight_words, weight_scales, bias, 
     with ExitStack() as stack:
         keep = stack.enter_context(tc.tile_pool(name="keep", bufs=1))
         prep = stack.enter_context(tc.tile_pool(name="prep", bufs=2))
-        evens = stack.enter_context(tc.tile_pool(name="evens", bufs=6))
+        evens = stack.enter_context(tc.tile_pool(name="evens", bufs=3))
         sums = stack.enter_context(tc.tile_pool(name="sums", bufs=3))
-        outs = stack.enter_context(tc.tile_pool(name="outs", bufs=4))
+        outs = stack.enter_context(tc.tile_pool(name="outs", bufs=3))
         psum = stack.enter_context(tc.psum_pool(name="psum", bufs=8))
         stack.enter_context(tc.manual_schedule())
 
@@ -137,36 +137,48 @@ def tile_iwht2layer_pa_t_e_kernel(tc, trans, weight_words, weight_scales, bias, 
                                     start=(v == 0),
                                     stop=(v == BLK - 1),
                                 )
-                            if u % 2 == 0:
-                                scaled = evens.tile([P, N_TILE], F32)
-                                if u == 0:
-                                    nc.vector.scalar_tensor_tensor(
-                                        out=scaled[:], in0=part[:], scalar=1.0 / COEFFS,
-                                        in1=bias_rows[:, cols], op0=MULT, op1=ADD,
-                                    )
-                                else:
-                                    nc.scalar.mul(out=scaled[:], in_=part[:], mul=1.0 / COEFFS)
-                                even[j] = scaled
+                            if u == 0:
+                                biased = evens.tile([P, N_TILE], F32)
+                                nc.vector.scalar_tensor_tensor(
+                                    out=biased[:], in0=part[:], scalar=1.0 / COEFFS,
+                                    in1=bias_rows[:, cols], op0=MULT, op1=ADD,
+                                )
+                                even[j] = biased
+                            elif u == 1:
+                                first = sums.tile([P, 2, N_TILE], F32)
+                                nc.vector.scalar_tensor_tensor(
+                                    out=first[:, 0, :], in0=part[:], scalar=1.0 / COEFFS,
+                                    in1=even[j][:], op0=MULT, op1=ADD,
+                                )
+                                nc.vector.scalar_tensor_tensor(
+                                    out=first[:, 1, :], in0=part[:], scalar=-1.0 / COEFFS,
+                                    in1=even[j][:], op0=MULT, op1=ADD,
+                                )
+                                stage_a[(j, 0)] = first
+                            elif u == 2:
+                                signed = evens.tile([P, 2, N_TILE], F32)
+                                nc.scalar.mul(out=signed[:, 0, :], in_=part[:], mul=1.0 / COEFFS)
+                                nc.scalar.mul(out=signed[:, 1, :], in_=part[:], mul=-1.0 / COEFFS)
+                                even[j] = signed
                             else:
-                                both = sums.tile([P, 2, N_TILE], F32, tag="stage_a%d" % (u // 2))
+                                second = sums.tile([P, 2, N_TILE], F32)
                                 nc.vector.scalar_tensor_tensor(
-                                    out=both[:, 0, :], in0=part[:], scalar=1.0 / COEFFS,
-                                    in1=even[j][:], op0=MULT, op1=ADD,
+                                    out=second[:], in0=part[:].unsqueeze(1).to_broadcast([P, 2, N_TILE]),
+                                    scalar=1.0 / COEFFS, in1=even[j][:], op0=MULT, op1=ADD,
                                 )
-                                nc.vector.scalar_tensor_tensor(
-                                    out=both[:, 1, :], in0=part[:], scalar=-1.0 / COEFFS,
-                                    in1=even[j][:], op0=MULT, op1=ADD,
-                                )
-                                stage_a[(j, u // 2)] = both
+                                stage_a[(j, 1)] = second
                     for j in range(first_j, first_j + J_GROUP):
-                        upper = outs.tile([P, 2, N_TILE], F32)
-                        lower = outs.tile([P, 2, N_TILE], F32)
-                        nc.vector.tensor_tensor(
-                            out=upper[:], in0=stage_a[(j, 0)][:], in1=stage_a[(j, 1)][:], op=ADD
+                        plus = outs.tile([P, 2, N_TILE], F32)
+                        minus = outs.tile([P, 2, N_TILE], F32)
+                        adder = nc.gpsimd if j == 0 else nc.vector
+                        adder.tensor_tensor(
+                            out=plus[:], in0=stage_a[(j, 0)][:], in1=stage_a[(j, 1)][:], op=ADD
                         )
                         nc.gpsimd.tensor_tensor(
-                            out=lower[:], in0=stage_a[(j, 0)][:], in1=stage_a[(j, 1)][:], op=SUBTRACT
+                            out=minus[:], in0=stage_a[(j, 0)][:], in1=stage_a[(j, 1)][:], op=SUBTRACT
                         )
-                        for i in range(BLK):
-                            pixels = (upper, lower)[i // 2]
-                            nc.sync.dma_start(out=out_dram[i, j, m, :, :, cols], in_=pixels[:, i % 2, :])
+                        for pixels, pixel_rows in ((plus, (0, 3)), (minus, (2, 1))):
+                            for half in range(2):
+                                nc.sync.dma_start(
+                                    out=out_dram[pixel_rows[half], j, m, :, :, cols], in_=pixels[:, half, :]
+                                )

@@ -43,7 +43,7 @@ def tile_iwht2layer_pa_t_e_kernel(tc, trans, weight_words, weight_scales, bias, 
         keep = stack.enter_context(tc.tile_pool(name="keep", bufs=1))
         prep = stack.enter_context(tc.tile_pool(name="prep", bufs=2))
         evens = stack.enter_context(tc.tile_pool(name="evens", bufs=3))
-        sums = stack.enter_context(tc.tile_pool(name="sums", bufs=3))
+        sums = stack.enter_context(tc.tile_pool(name="sums", bufs=4))
         outs = stack.enter_context(tc.tile_pool(name="outs", bufs=3))
         psum = stack.enter_context(tc.psum_pool(name="psum", bufs=8))
         stack.enter_context(tc.manual_schedule())
@@ -117,68 +117,86 @@ def tile_iwht2layer_pa_t_e_kernel(tc, trans, weight_words, weight_scales, bias, 
             nc.tensor.matmul(out=spread[:], lhsT=ones[:], rhs=bias_row0[:, cols], start=True, stop=True)
             nc.scalar.copy(out=bias_rows[:, cols], in_=spread[:])
 
-        for n in range(COL_TILES):
+        def store(n, m, j, pixels, pixel_rows):
             cols = slice(n * N_TILE, (n + 1) * N_TILE)
+            for half in range(2):
+                nc.sync.dma_start(out=out_dram[pixel_rows[half], j, m, :, :, cols], in_=pixels[:, half, :])
+
+        def second_stage(n, m, js, stage_a, last, helper_sums):
+            sums_of = {}
+            for j in js:
+                if j not in helper_sums:
+                    plus = outs.tile([P, 2, N_TILE], F32, name="plus")
+                    nc.vector.tensor_tensor(out=plus[:], in0=stage_a[(j, 0)][:], in1=stage_a[(j, 1)][:], op=ADD)
+                    sums_of[j] = plus
+            for j in reversed(js):
+                if j in helper_sums:
+                    plus = outs.tile([P, 2, N_TILE], F32, name="plus")
+                    nc.gpsimd.tensor_tensor(out=plus[:], in0=stage_a[(j, 0)][:], in1=stage_a[(j, 1)][:], op=ADD)
+                    sums_of[j] = plus
+                minus_engine = nc.vector if last else nc.gpsimd
+                minus_engine.tensor_tensor(
+                    out=stage_a[(j, 1)][:], in0=stage_a[(j, 0)][:], in1=stage_a[(j, 1)][:], op=SUBTRACT
+                )
+            for j in reversed(js):
+                store(n, m, j, sums_of[j], (0, 3))
+                store(n, m, j, stage_a[(j, 1)], (2, 1))
+
+        groups = []
+        for n in range(COL_TILES):
             for m in range(ROW_TILES):
-                for first_j in range(0, BLK, J_GROUP):
-                    even = {}
-                    stage_a = {}
-                    for u in range(BLK):
-                        for j in range(first_j, first_j + J_GROUP):
-                            part = psum.tile([P, N_TILE], F32, tag="bank")
-                            for v in range(BLK):
-                                sign = PLUS if HADAMARD[j][v] > 0 else MINUS
-                                nc.tensor.matmul_mx(
-                                    out=part[:],
-                                    lhsT=x_codes[:, m, u, sign, v, :].bitcast(FP8X4),
-                                    lhsT_scale=x_scales[:, m, u, sign, v, :],
-                                    rhs=w_codes[:, BLK * u + v, cols].bitcast(FP8X4),
-                                    rhs_scale=w_scales[PACK * v : P, u, cols],
-                                    start=(v == 0),
-                                    stop=(v == BLK - 1),
-                                )
-                            if u == 0:
-                                biased = evens.tile([P, N_TILE], F32)
-                                nc.vector.scalar_tensor_tensor(
-                                    out=biased[:], in0=part[:], scalar=1.0 / COEFFS,
-                                    in1=bias_rows[:, cols], op0=MULT, op1=ADD,
-                                )
-                                even[j] = biased
-                            elif u == 1:
-                                first = sums.tile([P, 2, N_TILE], F32)
-                                nc.vector.scalar_tensor_tensor(
-                                    out=first[:, 0, :], in0=part[:], scalar=1.0 / COEFFS,
-                                    in1=even[j][:], op0=MULT, op1=ADD,
-                                )
-                                nc.vector.scalar_tensor_tensor(
-                                    out=first[:, 1, :], in0=part[:], scalar=-1.0 / COEFFS,
-                                    in1=even[j][:], op0=MULT, op1=ADD,
-                                )
-                                stage_a[(j, 0)] = first
-                            elif u == 2:
-                                signed = evens.tile([P, 2, N_TILE], F32)
-                                nc.scalar.mul(out=signed[:, 0, :], in_=part[:], mul=1.0 / COEFFS)
-                                nc.scalar.mul(out=signed[:, 1, :], in_=part[:], mul=-1.0 / COEFFS)
-                                even[j] = signed
-                            else:
-                                second = sums.tile([P, 2, N_TILE], F32)
-                                nc.vector.scalar_tensor_tensor(
-                                    out=second[:], in0=part[:].unsqueeze(1).to_broadcast([P, 2, N_TILE]),
-                                    scalar=1.0 / COEFFS, in1=even[j][:], op0=MULT, op1=ADD,
-                                )
-                                stage_a[(j, 1)] = second
-                    for j in range(first_j, first_j + J_GROUP):
-                        plus = outs.tile([P, 2, N_TILE], F32)
-                        minus = outs.tile([P, 2, N_TILE], F32)
-                        adder = nc.gpsimd if j == 0 else nc.vector
-                        adder.tensor_tensor(
-                            out=plus[:], in0=stage_a[(j, 0)][:], in1=stage_a[(j, 1)][:], op=ADD
+                if n == COL_TILES - 1 and m == ROW_TILES - 1:
+                    groups.extend([(n, m, (0, 1)), (n, m, (2,)), (n, m, (3,))])
+                else:
+                    groups.extend([(n, m, (0, 1)), (n, m, (2, 3))])
+
+        for index, (n, m, js) in enumerate(groups):
+            cols = slice(n * N_TILE, (n + 1) * N_TILE)
+            last = index == len(groups) - 1
+            even = {}
+            stage_a = {}
+            for u in range(BLK):
+                for j in js:
+                    part = psum.tile([P, N_TILE], F32, tag="bank")
+                    for v in range(BLK):
+                        sign = PLUS if HADAMARD[j][v] > 0 else MINUS
+                        nc.tensor.matmul_mx(
+                            out=part[:],
+                            lhsT=x_codes[:, m, u, sign, v, :].bitcast(FP8X4),
+                            lhsT_scale=x_scales[:, m, u, sign, v, :],
+                            rhs=w_codes[:, BLK * u + v, cols].bitcast(FP8X4),
+                            rhs_scale=w_scales[PACK * v : P, u, cols],
+                            start=(v == 0),
+                            stop=(v == BLK - 1),
                         )
-                        nc.gpsimd.tensor_tensor(
-                            out=minus[:], in0=stage_a[(j, 0)][:], in1=stage_a[(j, 1)][:], op=SUBTRACT
+                    if u == 0:
+                        biased = evens.tile([P, N_TILE], F32)
+                        nc.vector.scalar_tensor_tensor(
+                            out=biased[:], in0=part[:], scalar=1.0 / COEFFS,
+                            in1=bias_rows[:, cols], op0=MULT, op1=ADD,
                         )
-                        for pixels, pixel_rows in ((plus, (0, 3)), (minus, (2, 1))):
-                            for half in range(2):
-                                nc.sync.dma_start(
-                                    out=out_dram[pixel_rows[half], j, m, :, :, cols], in_=pixels[:, half, :]
-                                )
+                        even[j] = biased
+                    elif u == 1:
+                        first = sums.tile([P, 2, N_TILE], F32)
+                        nc.vector.scalar_tensor_tensor(
+                            out=first[:, 0, :], in0=part[:], scalar=1.0 / COEFFS,
+                            in1=even[j][:], op0=MULT, op1=ADD,
+                        )
+                        nc.vector.scalar_tensor_tensor(
+                            out=first[:, 1, :], in0=part[:], scalar=-1.0 / COEFFS,
+                            in1=even[j][:], op0=MULT, op1=ADD,
+                        )
+                        stage_a[(j, 0)] = first
+                    elif u == 2:
+                        signed = evens.tile([P, 2, N_TILE], F32)
+                        nc.scalar.mul(out=signed[:, 0, :], in_=part[:], mul=1.0 / COEFFS)
+                        nc.scalar.mul(out=signed[:, 1, :], in_=part[:], mul=-1.0 / COEFFS)
+                        even[j] = signed
+                    else:
+                        second = sums.tile([P, 2, N_TILE], F32)
+                        nc.vector.scalar_tensor_tensor(
+                            out=second[:], in0=part[:].unsqueeze(1).to_broadcast([P, 2, N_TILE]),
+                            scalar=1.0 / COEFFS, in1=even[j][:], op0=MULT, op1=ADD,
+                        )
+                        stage_a[(j, 1)] = second
+            second_stage(n, m, js, stage_a, last, () if (n, m) == (COL_TILES - 1, ROW_TILES - 1) else (0,))

@@ -41,17 +41,21 @@ def tile_iwht2layer_pa_t_e_kernel(tc, trans, weight_words, weight_scales, bias, 
 
     with ExitStack() as stack:
         keep = stack.enter_context(tc.tile_pool(name="keep", bufs=1))
+        share = stack.enter_context(tc.tile_pool(name="share", bufs=1))
         prep = stack.enter_context(tc.tile_pool(name="prep", bufs=2))
-        evens = stack.enter_context(tc.tile_pool(name="evens", bufs=3))
-        sums = stack.enter_context(tc.tile_pool(name="sums", bufs=4))
-        outs = stack.enter_context(tc.tile_pool(name="outs", bufs=3))
+        biased_pool = stack.enter_context(tc.tile_pool(name="biased_pool", bufs=3))
+        signed_pool = stack.enter_context(tc.tile_pool(name="signed_pool", bufs=3))
+        first_pool = stack.enter_context(tc.tile_pool(name="first_pool", bufs=6))
+        second_pool = stack.enter_context(tc.tile_pool(name="second_pool", bufs=6))
+        outs = stack.enter_context(tc.tile_pool(name="outs", bufs=5))
         psum = stack.enter_context(tc.psum_pool(name="psum", bufs=8))
         stack.enter_context(tc.manual_schedule())
 
-        x_raw = keep.tile([P, COEFFS, ROW_TILES, CHANNELS], BF16)
+        x_raw = share.tile([P, COEFFS, ROW_TILES, CHANNELS], BF16, tag="big", align_bytes=64)
         x_codes = keep.tile([P, ROW_TILES, BLK, 2, BLK, P], U32, align_bytes=64)
         x_scales = keep.tile([P, ROW_TILES, BLK, 2, BLK, P], U8, align_bytes=64)
-        w_codes = keep.tile([P, COEFFS, OUT_CHANNELS], U32, align_bytes=64)
+        w_first = keep.tile([P, COEFFS, N_TILE], U32, align_bytes=64)
+        w_half = [w_first]
         w_scales = keep.tile([P, BLK, OUT_CHANNELS], U8, align_bytes=64)
         nc.vector.memset(w_scales[:].bitcast(I32), 0)
         identity = keep.tile([P, P], F32)
@@ -63,11 +67,14 @@ def tile_iwht2layer_pa_t_e_kernel(tc, trans, weight_words, weight_scales, bias, 
 
         nc.scalar.dma_start(out=bias_row0[0:1, :], in_=bias.rearrange("a b c n -> (a b c) n"))
 
-        for u in range(BLK):
-            coeffs = slice(BLK * u, BLK * (u + 1))
-            nc.sync.dma_start(
-                out=x_raw[:, coeffs].rearrange("p t m c -> p t (m c)"), in_=x_dram[:, coeffs, :]
-            )
+        def load_trans(u):
+            for first_v in range(0, BLK, 2):
+                coeffs = slice(BLK * u + first_v, BLK * u + first_v + 2)
+                nc.sync.dma_start(
+                    out=x_raw[:, coeffs].rearrange("p t m c -> p t (m c)"), in_=x_dram[:, coeffs, :]
+                )
+
+        def load_scales(u):
             for quadrant in range(P // QUADRANT):
                 nc.sync.dma_start(
                     out=w_scales[QUADRANT * quadrant : QUADRANT * quadrant + BLK * PACK, u, :].bitcast(I32),
@@ -75,54 +82,106 @@ def tile_iwht2layer_pa_t_e_kernel(tc, trans, weight_words, weight_scales, bias, 
                         BLK * u : BLK * (u + 1), PACK * quadrant : PACK * (quadrant + 1), :
                     ].bitcast(I32),
                 )
-        for n in range(COL_TILES):
-            for u in range(BLK):
-                coeffs = slice(BLK * u, BLK * (u + 1))
-                nc.sync.dma_start(
-                    out=w_codes[:, coeffs, n * N_TILE : (n + 1) * N_TILE].bitcast(I32),
-                    in_=w_dram[:, coeffs, n * N_TILE * PACK : (n + 1) * N_TILE * PACK].bitcast(I32),
-                )
+
+        def load_weight(n, u):
+            coeffs = slice(BLK * u, BLK * (u + 1))
+            nc.sync.dma_start(
+                out=w_half[n][:, coeffs, :].bitcast(I32),
+                in_=w_dram[:, coeffs, n * N_TILE * PACK : (n + 1) * N_TILE * PACK].bitcast(I32),
+            )
 
         for u in range(BLK):
-            for m in range(ROW_TILES):
-                grouped = prep.tile([P, 2, BLK, P, PACK], BF16, align_bytes=64)
-                for first_v in range(0, BLK, 2):
-                    flipped = psum.tile([P, 2, 2, P], F32, tag="bank")
-                    for c in range(2):
-                        words = x_raw[:, BLK * u + first_v + c, m, :].bitcast(F32)
-                        for e in range(2):
-                            nc.tensor.transpose(
-                                flipped[:, c, e, :], words[:, e : CHANNELS // 2 : 2], identity[:]
-                            )
-                    nc.scalar.copy(
-                        out=grouped[:, PLUS, first_v : first_v + 2].bitcast(F32),
-                        in_=flipped[:].rearrange("p c e r -> p c r e"),
-                    )
-                nc.vector.tensor_scalar_mul(
-                    out=grouped[:, MINUS].rearrange("p v r t -> p (v r t)"),
-                    in0=grouped[:, PLUS].rearrange("p v r t -> p (v r t)"),
-                    scalar1=-1.0,
+            load_trans(u)
+            load_scales(u)
+        for u in range(BLK):
+            load_weight(0, u)
+
+        def prepare(u, m):
+            grouped = prep.tile([P, 2, BLK, P, PACK], BF16, align_bytes=64, name="grouped")
+            for first_v in range(0, BLK, 2):
+                flipped = psum.tile([P, 2, 2, P], F32, tag="bank", name="flipped")
+                for c in range(2):
+                    words = x_raw[:, BLK * u + first_v + c, m, :].bitcast(F32)
+                    for e in range(2):
+                        nc.tensor.transpose(flipped[:, c, e, :], words[:, e : CHANNELS // 2 : 2], identity[:])
+                nc.scalar.copy(
+                    out=grouped[:, PLUS, first_v : first_v + 2].bitcast(F32),
+                    in_=flipped[:].rearrange("p c e r -> p c r e"),
                 )
-                for sign in (PLUS, MINUS):
-                    nc.vector.quantize_mx(
-                        out=x_codes[:, m, u, sign].rearrange("p v r -> p (v r)").bitcast(FP8X4),
-                        scales=x_scales[:, m, u, sign].rearrange("p v r -> p (v r)"),
-                        in_=grouped[:, sign].rearrange("p v r t -> p (v r t)"),
-                    )
+            nc.vector.tensor_scalar_mul(
+                out=grouped[:, MINUS].rearrange("p v r t -> p (v r t)"),
+                in0=grouped[:, PLUS].rearrange("p v r t -> p (v r t)"),
+                scalar1=-1.0,
+            )
+            for sign in (PLUS, MINUS):
+                nc.vector.quantize_mx(
+                    out=x_codes[:, m, u, sign].rearrange("p v r -> p (v r)").bitcast(FP8X4),
+                    scales=x_scales[:, m, u, sign].rearrange("p v r -> p (v r)"),
+                    in_=grouped[:, sign].rearrange("p v r t -> p (v r t)"),
+                )
 
         bias_rows = keep.tile([P, OUT_CHANNELS], F32)
-        for n in range(COL_TILES):
-            cols = slice(n * N_TILE, (n + 1) * N_TILE)
-            spread = psum.tile([P, N_TILE], F32, tag="bank")
-            nc.tensor.matmul(out=spread[:], lhsT=ones[:], rhs=bias_row0[:, cols], start=True, stop=True)
-            nc.scalar.copy(out=bias_rows[:, cols], in_=spread[:])
+
+        def spread_bias():
+            for n in range(COL_TILES):
+                cols = slice(n * N_TILE, (n + 1) * N_TILE)
+                spread = psum.tile([P, N_TILE], F32, tag="bank", name="spread")
+                nc.tensor.matmul(out=spread[:], lhsT=ones[:], rhs=bias_row0[:, cols], start=True, stop=True)
+                nc.scalar.copy(out=bias_rows[:, cols], in_=spread[:])
 
         def store(n, m, j, pixels, pixel_rows):
             cols = slice(n * N_TILE, (n + 1) * N_TILE)
             for half in range(2):
                 nc.sync.dma_start(out=out_dram[pixel_rows[half], j, m, :, :, cols], in_=pixels[:, half, :])
 
-        def second_stage(n, m, js, stage_a, last, helper_sums):
+        def first_stage(n, m, u, key, terms, with_bias, even, stage_a):
+            cols = slice(n * N_TILE, (n + 1) * N_TILE)
+            part = psum.tile([P, N_TILE], F32, tag="bank", name="part")
+            for index, (v, sign) in enumerate(terms):
+                nc.tensor.matmul_mx(
+                    out=part[:],
+                    lhsT=x_codes[:, m, u, sign, v, :].bitcast(FP8X4),
+                    lhsT_scale=x_scales[:, m, u, sign, v, :],
+                    rhs=w_half[n][:, BLK * u + v, :].bitcast(FP8X4),
+                    rhs_scale=w_scales[PACK * v : P, u, cols],
+                    start=(index == 0),
+                    stop=(index == len(terms) - 1),
+                )
+            if u == 0:
+                biased = biased_pool.tile([P, N_TILE], F32, name="biased")
+                if with_bias:
+                    nc.vector.scalar_tensor_tensor(
+                        out=biased[:], in0=part[:], scalar=1.0 / COEFFS,
+                        in1=bias_rows[:, cols], op0=MULT, op1=ADD,
+                    )
+                else:
+                    nc.scalar.mul(out=biased[:], in_=part[:], mul=1.0 / COEFFS)
+                even[key] = biased
+            elif u == 1:
+                first = first_pool.tile([P, 2, N_TILE], F32, name="first")
+                nc.vector.scalar_tensor_tensor(
+                    out=first[:, 0, :], in0=part[:], scalar=1.0 / COEFFS,
+                    in1=even[key][:], op0=MULT, op1=ADD,
+                )
+                nc.vector.scalar_tensor_tensor(
+                    out=first[:, 1, :], in0=part[:], scalar=-1.0 / COEFFS,
+                    in1=even[key][:], op0=MULT, op1=ADD,
+                )
+                stage_a[(key, 0)] = first
+            elif u == 2:
+                signed = signed_pool.tile([P, 2, N_TILE], F32, name="signed")
+                nc.scalar.mul(out=signed[:, 0, :], in_=part[:], mul=1.0 / COEFFS)
+                nc.scalar.mul(out=signed[:, 1, :], in_=part[:], mul=-1.0 / COEFFS)
+                even[key] = signed
+            else:
+                second = second_pool.tile([P, 2, N_TILE], F32, name="second")
+                nc.vector.scalar_tensor_tensor(
+                    out=second[:], in0=part[:].unsqueeze(1).to_broadcast([P, 2, N_TILE]),
+                    scalar=1.0 / COEFFS, in1=even[key][:], op0=MULT, op1=ADD,
+                )
+                stage_a[(key, 1)] = second
+
+        def second_stage(n, m, js, stage_a, helper_sums, helper_differences):
             sums_of = {}
             for j in js:
                 if j not in helper_sums:
@@ -134,69 +193,54 @@ def tile_iwht2layer_pa_t_e_kernel(tc, trans, weight_words, weight_scales, bias, 
                     plus = outs.tile([P, 2, N_TILE], F32, name="plus")
                     nc.gpsimd.tensor_tensor(out=plus[:], in0=stage_a[(j, 0)][:], in1=stage_a[(j, 1)][:], op=ADD)
                     sums_of[j] = plus
-                minus_engine = nc.vector if last else nc.gpsimd
+                minus_engine = nc.gpsimd if j in helper_differences else nc.vector
                 minus_engine.tensor_tensor(
                     out=stage_a[(j, 1)][:], in0=stage_a[(j, 0)][:], in1=stage_a[(j, 1)][:], op=SUBTRACT
                 )
+            ready = []
+            late = []
             for j in reversed(js):
-                store(n, m, j, sums_of[j], (0, 3))
-                store(n, m, j, stage_a[(j, 1)], (2, 1))
+                for pixels, pixel_rows, helped in (
+                    (sums_of[j], (0, 3), j in helper_sums),
+                    (stage_a[(j, 1)], (2, 1), j in helper_differences),
+                ):
+                    (late if helped else ready).append((n, m, j, pixels, pixel_rows))
+            return ready, late
 
-        groups = []
-        for n in range(COL_TILES):
+        def whole_terms(j):
+            return tuple((v, PLUS if HADAMARD[j][v] > 0 else MINUS) for v in range(BLK))
+
+        for u in range(BLK):
             for m in range(ROW_TILES):
-                if n == COL_TILES - 1 and m == ROW_TILES - 1:
-                    groups.extend([(n, m, (0, 1)), (n, m, (2,)), (n, m, (3,))])
-                else:
-                    groups.extend([(n, m, (0, 1)), (n, m, (2, 3))])
+                prepare(u, m)
+        spread_bias()
+        w_second = share.tile([P, COEFFS, N_TILE], U32, tag="big", align_bytes=64)
+        w_half.append(w_second)
+        for u in range(BLK):
+            load_weight(1, u)
 
-        for index, (n, m, js) in enumerate(groups):
-            cols = slice(n * N_TILE, (n + 1) * N_TILE)
-            last = index == len(groups) - 1
+        groups = (
+            (0, 0, (0, 1), (0,), (0, 1)),
+            (0, 0, (2, 3), (2,), (2, 3)),
+            (0, 1, (0, 1), (0,), (0, 1)),
+            (0, 1, (2, 3), (2,), (2, 3)),
+            (1, 0, (0, 1), (0,), (0, 1)),
+            (1, 0, (2, 3), (2,), (2, 3)),
+            (1, 1, (0, 1), (), (0, 1)),
+            (1, 1, (2,), (), (2,)),
+            (1, 1, (3,), (), ()),
+        )
+
+        waiting = []
+        for n, m, js, helper_sums, helper_differences in groups:
             even = {}
             stage_a = {}
             for u in range(BLK):
                 for j in js:
-                    part = psum.tile([P, N_TILE], F32, tag="bank")
-                    for v in range(BLK):
-                        sign = PLUS if HADAMARD[j][v] > 0 else MINUS
-                        nc.tensor.matmul_mx(
-                            out=part[:],
-                            lhsT=x_codes[:, m, u, sign, v, :].bitcast(FP8X4),
-                            lhsT_scale=x_scales[:, m, u, sign, v, :],
-                            rhs=w_codes[:, BLK * u + v, cols].bitcast(FP8X4),
-                            rhs_scale=w_scales[PACK * v : P, u, cols],
-                            start=(v == 0),
-                            stop=(v == BLK - 1),
-                        )
-                    if u == 0:
-                        biased = evens.tile([P, N_TILE], F32)
-                        nc.vector.scalar_tensor_tensor(
-                            out=biased[:], in0=part[:], scalar=1.0 / COEFFS,
-                            in1=bias_rows[:, cols], op0=MULT, op1=ADD,
-                        )
-                        even[j] = biased
-                    elif u == 1:
-                        first = sums.tile([P, 2, N_TILE], F32)
-                        nc.vector.scalar_tensor_tensor(
-                            out=first[:, 0, :], in0=part[:], scalar=1.0 / COEFFS,
-                            in1=even[j][:], op0=MULT, op1=ADD,
-                        )
-                        nc.vector.scalar_tensor_tensor(
-                            out=first[:, 1, :], in0=part[:], scalar=-1.0 / COEFFS,
-                            in1=even[j][:], op0=MULT, op1=ADD,
-                        )
-                        stage_a[(j, 0)] = first
-                    elif u == 2:
-                        signed = evens.tile([P, 2, N_TILE], F32)
-                        nc.scalar.mul(out=signed[:, 0, :], in_=part[:], mul=1.0 / COEFFS)
-                        nc.scalar.mul(out=signed[:, 1, :], in_=part[:], mul=-1.0 / COEFFS)
-                        even[j] = signed
-                    else:
-                        second = sums.tile([P, 2, N_TILE], F32)
-                        nc.vector.scalar_tensor_tensor(
-                            out=second[:], in0=part[:].unsqueeze(1).to_broadcast([P, 2, N_TILE]),
-                            scalar=1.0 / COEFFS, in1=even[j][:], op0=MULT, op1=ADD,
-                        )
-                        stage_a[(j, 1)] = second
-            second_stage(n, m, js, stage_a, last, () if (n, m) == (COL_TILES - 1, ROW_TILES - 1) else (0,))
+                    first_stage(n, m, u, j, whole_terms(j), True, even, stage_a)
+            ready, late = second_stage(n, m, js, stage_a, helper_sums, helper_differences)
+            for item in waiting + ready:
+                store(*item)
+            waiting = late
+        for item in waiting:
+            store(*item)

@@ -51,12 +51,12 @@ def tile_iwht2layer_pa_t_e_kernel(tc, trans, weight_words, weight_scales, bias, 
         psum = stack.enter_context(tc.psum_pool(name="psum", bufs=8))
         stack.enter_context(tc.manual_schedule())
 
-        x_raw = share.tile([P, COEFFS, ROW_TILES, CHANNELS], BF16, tag="big", align_bytes=64)
-        x_codes = keep.tile([P, ROW_TILES, BLK, 2, BLK, P], U32, align_bytes=64)
-        x_scales = keep.tile([P, ROW_TILES, BLK, 2, BLK, P], U8, align_bytes=64)
-        w_first = keep.tile([P, COEFFS, N_TILE], U32, align_bytes=64)
+        x_raw = share.tile([P, COEFFS, ROW_TILES, CHANNELS], BF16, tag="big", align_bytes=256)
+        x_codes = keep.tile([P, ROW_TILES, BLK, 2, BLK, P], U32, align_bytes=256)
+        x_scales = keep.tile([P, ROW_TILES, BLK, 2, BLK, P], U8, align_bytes=256)
+        w_first = keep.tile([P, COEFFS, N_TILE], U32, align_bytes=256)
         w_half = [w_first]
-        w_scales = keep.tile([P, BLK, OUT_CHANNELS], U8, align_bytes=64)
+        w_scales = keep.tile([P, BLK, OUT_CHANNELS], U8, align_bytes=256)
         nc.vector.memset(w_scales[:].bitcast(I32), 0)
         identity = keep.tile([P, P], F32)
         make_identity(nc, identity[:])
@@ -97,7 +97,7 @@ def tile_iwht2layer_pa_t_e_kernel(tc, trans, weight_words, weight_scales, bias, 
             load_weight(0, u)
 
         def prepare(u, m):
-            grouped = prep.tile([P, 2, BLK, P, PACK], BF16, align_bytes=64, name="grouped")
+            grouped = prep.tile([P, 2, BLK, P, PACK], BF16, align_bytes=256, name="grouped")
             for first_v in range(0, BLK, 2):
                 flipped = psum.tile([P, 2, 2, P], F32, tag="bank", name="flipped")
                 for c in range(2):
@@ -214,7 +214,7 @@ def tile_iwht2layer_pa_t_e_kernel(tc, trans, weight_words, weight_scales, bias, 
             for m in range(ROW_TILES):
                 prepare(u, m)
         spread_bias()
-        w_second = share.tile([P, COEFFS, N_TILE], U32, tag="big", align_bytes=64)
+        w_second = share.tile([P, COEFFS, N_TILE], U32, tag="big", align_bytes=256)
         w_half.append(w_second)
         for u in range(BLK):
             load_weight(1, u)

@@ -51,12 +51,12 @@ def tile_iwht2layer_pa_t_e_kernel(tc, trans, weight_words, weight_scales, bias, 
         psum = stack.enter_context(tc.psum_pool(name="psum", bufs=8))
         stack.enter_context(tc.manual_schedule())
 
-        x_raw = share.tile([P, COEFFS, ROW_TILES, CHANNELS], BF16, tag="big", align_bytes=256)
-        x_codes = keep.tile([P, ROW_TILES, BLK, 2, BLK, P], U32, align_bytes=256)
-        x_scales = keep.tile([P, ROW_TILES, BLK, 2, BLK, P], U8, align_bytes=256)
-        w_first = keep.tile([P, COEFFS, N_TILE], U32, align_bytes=256)
+        x_raw = share.tile([P, COEFFS, ROW_TILES, CHANNELS], BF16, tag="big", align_bytes=2048)
+        x_codes = keep.tile([P, ROW_TILES, BLK, 2, BLK, P], U32, align_bytes=2048)
+        x_scales = keep.tile([P, ROW_TILES, BLK, 2, BLK, P], U8, align_bytes=2048)
+        w_first = keep.tile([P, COEFFS, N_TILE], U32, align_bytes=2048)
         w_half = [w_first]
-        w_scales = keep.tile([P, BLK, OUT_CHANNELS], U8, align_bytes=256)
+        w_scales = keep.tile([P, BLK, OUT_CHANNELS], U8, align_bytes=2048)
         nc.vector.memset(w_scales[:].bitcast(I32), 0)
         identity = keep.tile([P, P], F32)
         make_identity(nc, identity[:])
@@ -97,7 +97,7 @@ def tile_iwht2layer_pa_t_e_kernel(tc, trans, weight_words, weight_scales, bias, 
             load_weight(0, u)
 
         def prepare(u, m):
-            grouped = prep.tile([P, 2, BLK, P, PACK], BF16, align_bytes=256, name="grouped")
+            grouped = prep.tile([P, 2, BLK, P, PACK], BF16, align_bytes=2048, name="grouped")
             for first_v in range(0, BLK, 2):
                 flipped = psum.tile([P, 2, 2, P], F32, tag="bank", name="flipped")
                 for c in range(2):
@@ -214,7 +214,7 @@ def tile_iwht2layer_pa_t_e_kernel(tc, trans, weight_words, weight_scales, bias, 
             for m in range(ROW_TILES):
                 prepare(u, m)
         spread_bias()
-        w_second = share.tile([P, COEFFS, N_TILE], U32, tag="big", align_bytes=256)
+        w_second = share.tile([P, COEFFS, N_TILE], U32, tag="big", align_bytes=2048)
         w_half.append(w_second)
         for u in range(BLK):
             load_weight(1, u)

from contextlib import ExitStack

import concourse.mybir as mybir
from concourse.masks import make_identity

F32 = mybir.dt.float32
BF16 = mybir.dt.bfloat16
I32 = mybir.dt.int32
U32 = mybir.dt.uint32
U8 = mybir.dt.uint8
FP8X4 = mybir.dt.float8_e4m3fn_x4
ADD = mybir.AluOpType.add
SUBTRACT = mybir.AluOpType.subtract
MULT = mybir.AluOpType.mult

P = 128
PACK = 4
BLK = 4
COEFFS = BLK * BLK
ROWS = 256
ROW_TILES = ROWS // P
CHANNELS = 512
OUT_CHANNELS = 1024
N_TILE = 512
COL_TILES = OUT_CHANNELS // N_TILE
QUADRANT = 32
HADAMARD = ((1, 1, 1, 1), (1, -1, 1, -1), (1, 1, -1, -1), (1, -1, -1, 1))
PLUS = 0
MINUS = 1
J_GROUP = 2

FLOPS = 2 * COEFFS * ROWS * CHANNELS * OUT_CHANNELS


def tile_iwht2layer_pa_t_e_kernel(tc, trans, weight_words, weight_scales, bias, out):
    nc = tc.nc

    x_dram = trans.rearrange("t b h (w m) c -> (b h w) t (m c)", m=ROW_TILES)
    w_dram = weight_words.rearrange("g p n t -> p g (n t)")
    out_dram = out.rearrange("b (h i) (w m j) n -> i j m (b h) w n", i=BLK, m=ROW_TILES, j=BLK)

    with ExitStack() as stack:
        keep = stack.enter_context(tc.tile_pool(name="keep", bufs=1))
        share = stack.enter_context(tc.tile_pool(name="share", bufs=1))
        prep = stack.enter_context(tc.tile_pool(name="prep", bufs=2))
        biased_pool = stack.enter_context(tc.tile_pool(name="biased_pool", bufs=3))
        signed_pool = stack.enter_context(tc.tile_pool(name="signed_pool", bufs=3))
        first_pool = stack.enter_context(tc.tile_pool(name="first_pool", bufs=6))
        second_pool = stack.enter_context(tc.tile_pool(name="second_pool", bufs=6))
        outs = stack.enter_context(tc.tile_pool(name="outs", bufs=5))
        psum = stack.enter_context(tc.psum_pool(name="psum", bufs=8))
        stack.enter_context(tc.manual_schedule())

        x_raw = share.tile([P, COEFFS, ROW_TILES, CHANNELS], BF16, tag="big", align_bytes=2048)
        x_codes = keep.tile([P, ROW_TILES, BLK, 2, BLK, P], U32, align_bytes=2048)
        x_scales = keep.tile([P, ROW_TILES, BLK, 2, BLK, P], U8, align_bytes=2048)
        w_first = keep.tile([P, COEFFS, N_TILE], U32, align_bytes=2048)
        w_half = [w_first]
        w_scales = keep.tile([P, BLK, OUT_CHANNELS], U8, align_bytes=2048)
        nc.vector.memset(w_scales[:].bitcast(I32), 0)
        identity = keep.tile([P, P], F32)
        make_identity(nc, identity[:])
        bias_row0 = keep.tile([P, OUT_CHANNELS], BF16)
        nc.gpsimd.memset(bias_row0[:], 0.0)
        ones = keep.tile([P, P], BF16)
        nc.gpsimd.memset(ones[:], 1.0)

        nc.scalar.dma_start(out=bias_row0[0:1, :], in_=bias.rearrange("a b c n -> (a b c) n"))

        def load_trans(u):
            for first_v in range(0, BLK, 2):
                coeffs = slice(BLK * u + first_v, BLK * u + first_v + 2)
                nc.sync.dma_start(
                    out=x_raw[:, coeffs].rearrange("p t m c -> p t (m c)"), in_=x_dram[:, coeffs, :]
                )

        def load_scales(u):
            for quadrant in range(P // QUADRANT):
                nc.sync.dma_start(
                    out=w_scales[QUADRANT * quadrant : QUADRANT * quadrant + BLK * PACK, u, :].bitcast(I32),
                    in_=weight_scales[
                        BLK * u : BLK * (u + 1), PACK * quadrant : PACK * (quadrant + 1), :
                    ].bitcast(I32),
                )

        def load_weight(n, u):
            coeffs = slice(BLK * u, BLK * (u + 1))
            nc.sync.dma_start(
                out=w_half[n][:, coeffs, :].bitcast(I32),
                in_=w_dram[:, coeffs, n * N_TILE * PACK : (n + 1) * N_TILE * PACK].bitcast(I32),
            )

        for u in range(BLK):
            load_trans(u)
            load_scales(u)
        for u in range(BLK):
            load_weight(0, u)

        def prepare(u, m):
            grouped = prep.tile([P, 2, BLK, P, PACK], BF16, align_bytes=2048, name="grouped")
            for first_v in range(0, BLK, 2):
                flipped = psum.tile([P, 2, 2, P], F32, tag="bank", name="flipped")
                for c in range(2):
                    words = x_raw[:, BLK * u + first_v + c, m, :].bitcast(F32)
                    for e in range(2):
                        nc.tensor.transpose(flipped[:, c, e, :], words[:, e : CHANNELS // 2 : 2], identity[:])
                nc.scalar.copy(
                    out=grouped[:, PLUS, first_v : first_v + 2].bitcast(F32),
                    in_=flipped[:].rearrange("p c e r -> p c r e"),
                )
            nc.vector.tensor_scalar_mul(
                out=grouped[:, MINUS].rearrange("p v r t -> p (v r t)"),
                in0=grouped[:, PLUS].rearrange("p v r t -> p (v r t)"),
                scalar1=-1.0,
            )
            for sign in (PLUS, MINUS):
                nc.vector.quantize_mx(
                    out=x_codes[:, m, u, sign].rearrange("p v r -> p (v r)").bitcast(FP8X4),
                    scales=x_scales[:, m, u, sign].rearrange("p v r -> p (v r)"),
                    in_=grouped[:, sign].rearrange("p v r t -> p (v r t)"),
                )

        bias_rows = keep.tile([P, OUT_CHANNELS], F32)

        def spread_bias():
            for n in range(COL_TILES):
                cols = slice(n * N_TILE, (n + 1) * N_TILE)
                spread = psum.tile([P, N_TILE], F32, tag="bank", name="spread")
                nc.tensor.matmul(out=spread[:], lhsT=ones[:], rhs=bias_row0[:, cols], start=True, stop=True)
                nc.scalar.copy(out=bias_rows[:, cols], in_=spread[:])

        def store(n, m, j, pixels, pixel_rows):
            cols = slice(n * N_TILE, (n + 1) * N_TILE)
            for half in range(2):
                nc.sync.dma_start(out=out_dram[pixel_rows[half], j, m, :, :, cols], in_=pixels[:, half, :])

        def first_stage(n, m, u, key, terms, with_bias, even, stage_a):
            cols = slice(n * N_TILE, (n + 1) * N_TILE)
            part = psum.tile([P, N_TILE], F32, tag="bank", name="part")
            for index, (v, sign) in enumerate(terms):
                nc.tensor.matmul_mx(
                    out=part[:],
                    lhsT=x_codes[:, m, u, sign, v, :].bitcast(FP8X4),
                    lhsT_scale=x_scales[:, m, u, sign, v, :],
                    rhs=w_half[n][:, BLK * u + v, :].bitcast(FP8X4),
                    rhs_scale=w_scales[PACK * v : P, u, cols],
                    start=(index == 0),
                    stop=(index == len(terms) - 1),
                )
            if u == 0:
                biased = biased_pool.tile([P, N_TILE], F32, name="biased")
                if with_bias:
                    nc.vector.scalar_tensor_tensor(
                        out=biased[:], in0=part[:], scalar=1.0 / COEFFS,
                        in1=bias_rows[:, cols], op0=MULT, op1=ADD,
                    )
                else:
                    nc.scalar.mul(out=biased[:], in_=part[:], mul=1.0 / COEFFS)
                even[key] = biased
            elif u == 1:
                first = first_pool.tile([P, 2, N_TILE], F32, name="first")
                nc.vector.scalar_tensor_tensor(
                    out=first[:, 0, :], in0=part[:], scalar=1.0 / COEFFS,
                    in1=even[key][:], op0=MULT, op1=ADD,
                )
                nc.vector.scalar_tensor_tensor(
                    out=first[:, 1, :], in0=part[:], scalar=-1.0 / COEFFS,
                    in1=even[key][:], op0=MULT, op1=ADD,
                )
                stage_a[(key, 0)] = first
            elif u == 2:
                signed = signed_pool.tile([P, 2, N_TILE], F32, name="signed")
                nc.scalar.mul(out=signed[:, 0, :], in_=part[:], mul=1.0 / COEFFS)
                nc.scalar.mul(out=signed[:, 1, :], in_=part[:], mul=-1.0 / COEFFS)
                even[key] = signed
            else:
                second = second_pool.tile([P, 2, N_TILE], F32, name="second")
                nc.vector.scalar_tensor_tensor(
                    out=second[:], in0=part[:].unsqueeze(1).to_broadcast([P, 2, N_TILE]),
                    scalar=1.0 / COEFFS, in1=even[key][:], op0=MULT, op1=ADD,
                )
                stage_a[(key, 1)] = second

        def second_stage(n, m, js, stage_a, helper_sums, helper_differences):
            sums_of = {}
            for j in js:
                if j not in helper_sums:
                    plus = outs.tile([P, 2, N_TILE], F32, name="plus")
                    nc.vector.tensor_tensor(out=plus[:], in0=stage_a[(j, 0)][:], in1=stage_a[(j, 1)][:], op=ADD)
                    sums_of[j] = plus
            for j in reversed(js):
                if j in helper_sums:
                    plus = outs.tile([P, 2, N_TILE], F32, name="plus")
                    nc.gpsimd.tensor_tensor(out=plus[:], in0=stage_a[(j, 0)][:], in1=stage_a[(j, 1)][:], op=ADD)
                    sums_of[j] = plus
                minus_engine = nc.gpsimd if j in helper_differences else nc.vector
                minus_engine.tensor_tensor(
                    out=stage_a[(j, 1)][:], in0=stage_a[(j, 0)][:], in1=stage_a[(j, 1)][:], op=SUBTRACT
                )
            ready = []
            late = []
            for j in reversed(js):
                for pixels, pixel_rows, helped in (
                    (sums_of[j], (0, 3), j in helper_sums),
                    (stage_a[(j, 1)], (2, 1), j in helper_differences),
                ):
                    (late if helped else ready).append((n, m, j, pixels, pixel_rows))
            return ready, late

        def whole_terms(j):
            return tuple((v, PLUS if HADAMARD[j][v] > 0 else MINUS) for v in range(BLK))

        for u in range(BLK):
            for m in range(ROW_TILES):
                prepare(u, m)
        spread_bias()
        w_second = share.tile([P, COEFFS, N_TILE], U32, tag="big", align_bytes=2048)
        w_half.append(w_second)
        for u in range(BLK):
            load_weight(1, u)

        groups = (
            (0, 0, (0, 1), (0,), (0, 1)),
            (0, 0, (2, 3), (2,), (2, 3)),
            (0, 1, (0, 1), (0,), (0, 1)),
            (0, 1, (2, 3), (2,), (2, 3)),
            (1, 0, (0, 1), (0,), (0, 1)),
            (1, 0, (2, 3), (2,), (2, 3)),
            (1, 1, (0, 1), (), (0, 1)),
            (1, 1, (2,), (), (2,)),
            (1, 1, (3,), (), ()),
        )

        waiting = []
        for n, m, js, helper_sums, helper_differences in groups:
            even = {}
            stage_a = {}
            for u in range(BLK):
                for j in js:
                    first_stage(n, m, u, j, whole_terms(j), True, even, stage_a)
            ready, late = second_stage(n, m, js, stage_a, helper_sums, helper_differences)
            for item in waiting + ready:
                store(*item)
            waiting = late
        for item in waiting:
            store(*item)
